import numpy as np
import ml_dtypes


def mxq(x, axis, fmt="e4m3"):
    dtype, down = {"e4m3": (ml_dtypes.float8_e4m3fn, 7), "e5m2": (ml_dtypes.float8_e5m2, 14)}[fmt]
    v = np.moveaxis(np.asarray(x, np.float32).astype(ml_dtypes.bfloat16).astype(np.float64), axis, -1)
    blocks = v.reshape(v.shape[:-1] + (-1, 32))
    amax = np.abs(blocks).max(-1, keepdims=True)
    byte = np.maximum(np.where(amax > 0, np.frexp(amax)[1] - 1 + 127, 0) - down, 1)
    scale = np.exp2(byte - 127.0)
    codes = (blocks / scale).astype(np.float32).astype(dtype).astype(np.float64)
    return np.moveaxis((codes * scale).reshape(v.shape), -1, axis)


WIDE = False


def mx_kscale(k):
    if not WIDE:
        return np.ones(k)
    levels = np.array([10, -10, 5, -5, 0])
    a = np.random.permutation(np.resize(levels, k // 512 * 4)).reshape(k // 512, 4)
    idx = np.arange(k)
    return np.exp2(a[idx // 512, idx % 128 // 32])


BF16 = ml_dtypes.bfloat16


def bf(x):
    return np.asarray(x, np.float32).astype(BF16)


def f64(x):
    return np.asarray(x).astype(np.float64)


E2M1 = np.array([0.0, 0.5, 1.0, 1.5, 2.0, 3.0, 4.0, 6.0, -0.0, -0.5, -1.0, -1.5, -2.0, -3.0, -4.0, -6.0])


def pack_weight(w, fmt):
    k, n = w.shape
    w = f64(bf(w)).reshape(k // 32, 32, n)
    amax = np.abs(w).max(1)
    if fmt == "e4m3":
        byte = np.frexp(amax)[1] - 1 + 127 - 7
    else:
        mant, ex = np.frexp(amax / 6.0)
        byte = np.where(mant > 0.5, ex, ex - 1) + 127
    byte = np.clip(np.where(amax > 0, byte, 1), 1, 254)
    scaled = (w * np.exp2(127.0 - byte)[:, None, :]).reshape(k, n).astype(np.float32)
    by_word = np.ascontiguousarray(scaled.reshape(k // 512, 128, 4, n).transpose(0, 1, 3, 2))
    if fmt == "e4m3":
        words = by_word.astype(ml_dtypes.float8_e4m3fn).view(np.uint8)
    else:
        c = by_word.astype(ml_dtypes.float4_e2m1fn).view(np.uint8) & 0xF
        words = c[..., 0::2] | (c[..., 1::2] << 4)
    return np.ascontiguousarray(words), np.ascontiguousarray(byte.astype(np.uint8).reshape(k // 512, 16, n))


def unpack_weight(words, scales, fmt):
    g, p, n, _ = words.shape
    if fmt == "e4m3":
        vals = np.ascontiguousarray(words).view(ml_dtypes.float8_e4m3fn).astype(np.float64)
    else:
        nib = np.empty((g, p, n, 4), np.uint8)
        nib[..., 0::2] = words & 0xF
        nib[..., 1::2] = words >> 4
        vals = E2M1[nib]
    vals = vals * np.repeat(np.exp2(scales.astype(np.float64) - 127.0), 8, axis=1)[..., None]
    return vals.transpose(0, 1, 3, 2).reshape(g * 512, n)


B, N, NI, NH, NO = 1, 128, 2048, 1024, 2
CONTEXT = 3
H = NH * CONTEXT


def _shift(x, d):
    if d == 0:
        return x
    if d > 0:
        return np.pad(x[:, d:, :], ((0, 0), (0, d), (0, 0)))
    return np.pad(x[:, :d, :], ((0, 0), (-d, 0), (0, 0)))


def setup_inputs():
    u = mx_kscale(NH)
    uu = np.tile(u, CONTEXT)
    x = bf(np.random.standard_normal((B, N, NI)))
    W_lin = bf(np.random.standard_normal((NI, NH)) / np.sqrt(NI) * u)
    b_lin = bf(np.random.standard_normal(NH) * 0.3 * u)
    stack = np.random.standard_normal((NO, H, H)) * 8.0 / H / uu[:, None] / uu[None, :]
    words, scales = pack_weight(stack.reshape(-1, H), "e4m3")
    b_bil = bf(np.random.standard_normal(NO))
    return {"x": x,
            "W_lin": W_lin,
            "b_lin": b_lin,
            "W_bil_words": words,
            "W_bil_scales": scales,
            "b_bil": b_bil}


def reference(x, W_lin, b_lin, W_bil_words, W_bil_scales, b_bil):
    h = np.maximum(f64(x) @ f64(W_lin) + f64(b_lin), 0.0)
    hq = mxq(h, 2, "e4m3")
    w = CONTEXT // 2
    wr = unpack_weight(W_bil_words, W_bil_scales, "e4m3").reshape(NO, H, H).reshape(NO, CONTEXT, NH, H).transpose(2, 1, 0, 3).reshape(NH, CONTEXT * NO * H)
    p = (hq @ wr).reshape(B, N, CONTEXT, NO * H)
    t = sum(_shift(p[:, :, c, :], c - w) for c in range(CONTEXT))
    tr = t.reshape(B, N * NO * CONTEXT, NH).transpose(0, 2, 1)
    q = (hq @ mxq(tr, 1, "e4m3")).reshape(B, N, N * NO, CONTEXT)
    o = sum(_shift(q[:, :, :, c], c - w) for c in range(CONTEXT))
    return o.reshape(B, N, N, NO).transpose(0, 2, 1, 3) + f64(b_bil)

@@ -1,0 +1,243 @@
+from contextlib import ExitStack
+
+import concourse.mybir as mybir
+from concourse.masks import make_identity
+
+BF16 = mybir.dt.bfloat16
+F32 = mybir.dt.float32
+I32 = mybir.dt.int32
+U32 = mybir.dt.uint32
+U8 = mybir.dt.uint8
+FP8X4 = mybir.dt.float8_e4m3fn_x4
+
+P = 128
+PACK = 4
+K_PASS = P * PACK
+
+SEQ = 128
+NI = 2048
+NH = 1024
+NO = 2
+CONTEXT = 3
+H = NH * CONTEXT
+
+H_PASSES = NH // K_PASS
+V_PASSES = H // K_PASS
+UNITS = H // K_PASS
+UNITS_PER_LOAD = 3
+LIN_BLOCKS = NI // P
+BANK = 512
+PLANES_PER_TILE = 4
+
+BY_WORD = 0
+BY_TILE = 1
+
+FLOPS = 2 * SEQ * NI * NH + 2 * SEQ * H * H * NO + 2 * SEQ * SEQ * H * NO
+
+
+def plan_loads():
+    loads = []
+    for o in range(NO):
+        for first in range(0, UNITS, UNITS_PER_LOAD):
+            is_last = o == NO - 1 and first == UNITS - UNITS_PER_LOAD
+            step = 1 if is_last else UNITS_PER_LOAD
+            for start in range(first, first + UNITS_PER_LOAD, step):
+                loads.append((o, start, step))
+    return loads
+
+
+def tile_bilinearpairedlayer_w_e_kernel(
+    tc, x, W_lin, b_lin, W_bil_words, W_bil_scales, b_bil, out
+):
+    nc = tc.nc
+    with ExitStack() as ctx:
+        keep = ctx.enter_context(tc.tile_pool(name="keep", bufs=1))
+        stage = ctx.enter_context(tc.tile_pool(name="stage", bufs=3))
+        psum_flip = ctx.enter_context(tc.psum_pool(name="psum_flip", bufs=2))
+        psum_h = ctx.enter_context(tc.psum_pool(name="psum_h", bufs=1))
+        psum_t = ctx.enter_context(tc.psum_pool(name="psum_t", bufs=3))
+        psum_out = ctx.enter_context(tc.psum_pool(name="psum_out", bufs=1))
+
+        planes = keep.tile([P, NO * V_PASSES // PLANES_PER_TILE, H], U8, align_bytes=64)
+        nc.vector.memset(planes[:].rearrange("p a n -> p (a n)").bitcast(I32), 0)
+        ident = keep.tile([P, P], BF16)
+        make_identity(nc, ident[:])
+        bias_rows = keep.tile([P, NH], BF16)
+        nc.gpsimd.memset(bias_rows[:], 0.0)
+        ones = keep.tile([P, P], BF16)
+        nc.gpsimd.memset(ones[:], 1.0)
+        v_grouped = keep.tile([P, 2, CONTEXT, H_PASSES, SEQ, PACK], BF16, align_bytes=64)
+        nc.vector.memset(v_grouped[:, :, 0, :, 0, :], 0.0)
+        nc.vector.memset(v_grouped[:, :, 2, :, SEQ - 1, :], 0.0)
+
+        x_sb = keep.tile([P, NI], BF16)
+        nc.sync.dma_start(out=x_sb[:], in_=x[0])
+        nc.scalar.dma_start(out=bias_rows[0:1, :], in_=b_lin.unsqueeze(0))
+        b_bil_bf = keep.tile([P, NO], BF16)
+        nc.scalar.dma_start(out=b_bil_bf[:], in_=b_bil.partition_broadcast(P))
+        b_bil_f32 = keep.tile([P, NO], F32)
+        nc.vector.tensor_copy(out=b_bil_f32[:], in_=b_bil_bf[:])
+
+        w_lin_sb = keep.tile([P, NI // K_PASS, PACK, NH], BF16)
+        for b in range(NI // K_PASS):
+            nc.sync.dma_start(
+                out=w_lin_sb[:, b].rearrange("p j k -> p (j k)"),
+                in_=W_lin[K_PASS * b : K_PASS * (b + 1), :].rearrange("(p j) k -> p (j k)", j=PACK),
+            )
+
+        for a in range(NO * V_PASSES // PLANES_PER_TILE):
+            for quad in range(4):
+                nc.sync.dma_start(
+                    out=planes[32 * quad : 32 * quad + 16, a, :].bitcast(I32),
+                    in_=W_bil_scales[
+                        PLANES_PER_TILE * a : PLANES_PER_TILE * (a + 1), 4 * quad : 4 * quad + 4, :
+                    ].bitcast(I32),
+                )
+
+        words_dram = W_bil_words.rearrange("g p n t -> p g (n t)")
+        w_of_unit = {}
+        for o, first, units in plan_loads():
+            w_sb = keep.tile(
+                [P, V_PASSES, units * K_PASS * PACK], U8, name="w_%d_%d" % (o, first), align_bytes=64
+            )
+            nc.sync.dma_start(
+                out=w_sb[:].bitcast(I32),
+                in_=words_dram[
+                    :,
+                    V_PASSES * o : V_PASSES * (o + 1),
+                    first * K_PASS * PACK : (first + units) * K_PASS * PACK,
+                ].bitcast(I32),
+            )
+            for unit in range(first, first + units):
+                w_of_unit[(o, unit)] = (w_sb, first)
+
+        x_cols = x_sb[:].rearrange("i (b p j) -> i b j p", p=P, j=PACK)
+        xT_sb = keep.tile([P, LIN_BLOCKS, SEQ], BF16)
+        per_bank = LIN_BLOCKS // 2
+        for half in range(2):
+            xT_ps = psum_flip.tile([P, per_bank, SEQ], BF16, tag="flip")
+            for s in range(per_bank):
+                b, j = divmod(per_bank * half + s, PACK)
+                nc.tensor.transpose(xT_ps[:, s, :], x_cols[:, b, j, :], ident[:])
+            if half == 0:
+                nc.vector.tensor_copy(out=xT_sb[:, 0:per_bank, :], in_=xT_ps[:])
+            else:
+                nc.scalar.copy(out=xT_sb[:, per_bank:LIN_BLOCKS, :], in_=xT_ps[:])
+
+        h_ps = [psum_h.tile([P, BANK], F32, name="h_ps%d" % n) for n in range(NH // BANK)]
+        for n in range(NH // BANK):
+            nc.tensor.matmul(
+                h_ps[n][:], lhsT=ones[:], rhs=bias_rows[:, BANK * n : BANK * (n + 1)],
+                start=True, stop=False,
+            )
+        for block in range(LIN_BLOCKS):
+            b, j = divmod(block, PACK)
+            for n in range(NH // BANK):
+                nc.tensor.matmul(
+                    h_ps[n][:],
+                    lhsT=xT_sb[:, block, :],
+                    rhs=w_lin_sb[:, b, j, BANK * n : BANK * (n + 1)],
+                    start=False,
+                    stop=(block == LIN_BLOCKS - 1),
+                )
+        h_sb = keep.tile([P, NH], BF16)
+        nc.scalar.activation(
+            out=h_sb[:, 0:BANK], in_=h_ps[0][:], func=mybir.ActivationFunctionType.Relu
+        )
+        nc.vector.tensor_scalar_max(out=h_sb[:, BANK:NH], in0=h_ps[1][:], scalar1=0.0)
+
+        h_cols = (
+            h_sb[:].rearrange("i (g p t) -> i g t p", p=P, t=PACK),
+            h_sb[:].rearrange("i (g t p) -> i g t p", p=P, t=PACK),
+        )
+        v_words = keep.tile([P, 2, CONTEXT, H_PASSES, SEQ], U32, align_bytes=64)
+        v_scales = keep.tile([P, 2, CONTEXT, H_PASSES, SEQ], U8, align_bytes=64)
+        for order in (BY_WORD, BY_TILE):
+            hT_ps = psum_flip.tile([P, H_PASSES, PACK, SEQ], BF16, tag="flip")
+            for g in range(H_PASSES):
+                for t in range(PACK):
+                    nc.tensor.transpose(hT_ps[:, g, t, :], h_cols[order][:, g, t, :], ident[:])
+            centre = v_grouped[:, order, 1]
+            if order == BY_WORD:
+                nc.vector.tensor_copy(out=centre, in_=hT_ps[:].rearrange("p g t i -> p g i t"))
+            else:
+                nc.scalar.copy(out=centre, in_=hT_ps[:].rearrange("p g t i -> p g i t"))
+            nc.vector.tensor_copy(
+                out=v_grouped[:, order, 0, :, 1:SEQ, :], in_=centre[:, :, 0 : SEQ - 1, :]
+            )
+            nc.vector.tensor_copy(
+                out=v_grouped[:, order, 2, :, 0 : SEQ - 1, :], in_=centre[:, :, 1:SEQ, :]
+            )
+            for c in range(CONTEXT):
+                nc.vector.quantize_mx(
+                    out=v_words[:, order, c].rearrange("p g i -> p (g i)").bitcast(FP8X4),
+                    scales=v_scales[:, order, c].rearrange("p g i -> p (g i)"),
+                    in_=v_grouped[:, order, c].rearrange("p g i t -> p (g i t)"),
+                )
+
+        out_ps = psum_out.tile([P, NO, SEQ], F32)
+
+        def first_product(o, unit):
+            w_sb, first = w_of_unit[(o, unit)]
+            tT_ps = psum_t.tile([P, PACK, SEQ], F32)
+            for m in range(PACK):
+                col = K_PASS * unit + P * m
+                byte = (col - K_PASS * first) * PACK
+                for kp in range(V_PASSES):
+                    c, g = divmod(kp, H_PASSES)
+                    a, q = divmod(V_PASSES * o + kp, PLANES_PER_TILE)
+                    nc.tensor.matmul_mx(
+                        out=tT_ps[:, m, :],
+                        lhsT=w_sb[:, kp, byte : byte + P * PACK].bitcast(FP8X4),
+                        lhsT_scale=planes[4 * q : P, a, col : col + P],
+                        rhs=v_words[:, BY_WORD, c, g, :].bitcast(FP8X4),
+                        rhs_scale=v_scales[:, BY_WORD, c, g, :],
+                        start=(kp == 0),
+                        stop=(kp == V_PASSES - 1),
+                    )
+            return tT_ps
+
+        def quantise_t(tT_ps):
+            t_grouped = stage.tile([P, SEQ, PACK], BF16, align_bytes=64)
+            nc.scalar.copy(out=t_grouped[:], in_=tT_ps[:].rearrange("p m i -> p i m"))
+            t_words = stage.tile([P, SEQ], U32, align_bytes=64)
+            t_scales = stage.tile([P, SEQ], U8, align_bytes=64)
+            nc.vector.quantize_mx(
+                out=t_words[:].bitcast(FP8X4),
+                scales=t_scales[:],
+                in_=t_grouped[:].rearrange("p i m -> p (i m)"),
+            )
+            return t_words, t_scales
+
+        def second_product(o, unit, t_words, t_scales):
+            c, g = divmod(unit, H_PASSES)
+            nc.tensor.matmul_mx(
+                out=out_ps[:, o, :],
+                lhsT=t_words[:].bitcast(FP8X4),
+                lhsT_scale=t_scales[:],
+                rhs=v_words[:, BY_TILE, c, g, :].bitcast(FP8X4),
+                rhs_scale=v_scales[:, BY_TILE, c, g, :],
+                start=(unit == 0),
+                stop=(unit == UNITS - 1),
+            )
+
+        waiting = None
+        for o in range(NO):
+            for unit in range(UNITS):
+                tT_ps = first_product(o, unit)
+                t_words, t_scales = quantise_t(tT_ps)
+                if waiting is not None:
+                    second_product(*waiting)
+                waiting = (o, unit, t_words, t_scales)
+        second_product(*waiting)
+
+        result = keep.tile([P, SEQ, NO], F32)
+        nc.vector.tensor_tensor(
+            out=result[:],
+            in0=out_ps[:].rearrange("i o j -> i j o"),
+            in1=b_bil_f32[:].unsqueeze(1).to_broadcast([P, SEQ, NO]),
+            op=mybir.AluOpType.add,
+        )
+        nc.sync.dma_start(
+            out=out[0].rearrange("i j o -> i (j o)"), in_=result[:].rearrange("i j o -> i (j o)")
+        )

@@ -24,7 +24,6 @@ H = NH * CONTEXT
 H_PASSES = NH // K_PASS
 V_PASSES = H // K_PASS
 UNITS = H // K_PASS
-UNITS_PER_LOAD = 3
 LIN_BLOCKS = NI // P
 BANK = 512
 PLANES_PER_TILE = 4
@@ -35,17 +34,6 @@ BY_TILE = 1
 FLOPS = 2 * SEQ * NI * NH + 2 * SEQ * H * H * NO + 2 * SEQ * SEQ * H * NO
 
 
-def plan_loads():
-    loads = []
-    for o in range(NO):
-        for first in range(0, UNITS, UNITS_PER_LOAD):
-            is_last = o == NO - 1 and first == UNITS - UNITS_PER_LOAD
-            step = 1 if is_last else UNITS_PER_LOAD
-            for start in range(first, first + UNITS_PER_LOAD, step):
-                loads.append((o, start, step))
-    return loads
-
-
 def tile_bilinearpairedlayer_w_e_kernel(
     tc, x, W_lin, b_lin, W_bil_words, W_bil_scales, b_bil, out
 ):
@@ -53,10 +41,6 @@ def tile_bilinearpairedlayer_w_e_kernel(
     with ExitStack() as ctx:
         keep = ctx.enter_context(tc.tile_pool(name="keep", bufs=1))
         stage = ctx.enter_context(tc.tile_pool(name="stage", bufs=3))
-        psum_flip = ctx.enter_context(tc.psum_pool(name="psum_flip", bufs=2))
-        psum_h = ctx.enter_context(tc.psum_pool(name="psum_h", bufs=1))
-        psum_t = ctx.enter_context(tc.psum_pool(name="psum_t", bufs=3))
-        psum_out = ctx.enter_context(tc.psum_pool(name="psum_out", bufs=1))
 
         planes = keep.tile([P, NO * V_PASSES // PLANES_PER_TILE, H], U8, align_bytes=64)
         nc.vector.memset(planes[:].rearrange("p a n -> p (a n)").bitcast(I32), 0)
@@ -94,112 +78,117 @@ def tile_bilinearpairedlayer_w_e_kernel(
                     ].bitcast(I32),
                 )
 
-        words_dram = W_bil_words.rearrange("g p n t -> p g (n t)")
-        w_of_unit = {}
-        for o, first, units in plan_loads():
-            w_sb = keep.tile(
-                [P, V_PASSES, units * K_PASS * PACK], U8, name="w_%d_%d" % (o, first), align_bytes=64
-            )
-            nc.sync.dma_start(
-                out=w_sb[:].bitcast(I32),
-                in_=words_dram[
-                    :,
-                    V_PASSES * o : V_PASSES * (o + 1),
-                    first * K_PASS * PACK : (first + units) * K_PASS * PACK,
-                ].bitcast(I32),
-            )
-            for unit in range(first, first + units):
-                w_of_unit[(o, unit)] = (w_sb, first)
+        w_of = {}
+        for group in range(NO * V_PASSES):
+            units = 1 if group == NO * V_PASSES - 1 else UNITS
+            for first in range(0, UNITS, units):
+                w_sb = keep.tile(
+                    [P, units * K_PASS * PACK], U8, name="w_%d_%d" % (group, first), align_bytes=64
+                )
+                nc.sync.dma_start(
+                    out=w_sb[:].bitcast(I32),
+                    in_=W_bil_words[group].rearrange("p n t -> p (n t)")[
+                        :, first * K_PASS * PACK : (first + units) * K_PASS * PACK
+                    ].bitcast(I32),
+                )
+                for unit in range(first, first + units):
+                    w_of[(group, unit)] = (w_sb, first)
 
-        x_cols = x_sb[:].rearrange("i (b p j) -> i b j p", p=P, j=PACK)
-        xT_sb = keep.tile([P, LIN_BLOCKS, SEQ], BF16)
-        per_bank = LIN_BLOCKS // 2
-        for half in range(2):
-            xT_ps = psum_flip.tile([P, per_bank, SEQ], BF16, tag="flip")
-            for s in range(per_bank):
-                b, j = divmod(per_bank * half + s, PACK)
-                nc.tensor.transpose(xT_ps[:, s, :], x_cols[:, b, j, :], ident[:])
-            if half == 0:
-                nc.vector.tensor_copy(out=xT_sb[:, 0:per_bank, :], in_=xT_ps[:])
-            else:
-                nc.scalar.copy(out=xT_sb[:, per_bank:LIN_BLOCKS, :], in_=xT_ps[:])
+        with tc.psum_pool(name="psum_flip", bufs=2) as psum_flip, tc.psum_pool(
+            name="psum_h", bufs=1
+        ) as psum_h:
+            x_cols = x_sb[:].rearrange("i (b p j) -> i b j p", p=P, j=PACK)
+            xT_sb = keep.tile([P, LIN_BLOCKS, SEQ], BF16)
+            per_bank = LIN_BLOCKS // 2
+            for half in range(2):
+                xT_ps = psum_flip.tile([P, per_bank, SEQ], BF16, tag="flip")
+                for s in range(per_bank):
+                    b, j = divmod(per_bank * half + s, PACK)
+                    nc.tensor.transpose(xT_ps[:, s, :], x_cols[:, b, j, :], ident[:])
+                if half == 0:
+                    nc.vector.tensor_copy(out=xT_sb[:, 0:per_bank, :], in_=xT_ps[:])
+                else:
+                    nc.scalar.copy(out=xT_sb[:, per_bank:LIN_BLOCKS, :], in_=xT_ps[:])
 
-        h_ps = [psum_h.tile([P, BANK], F32, name="h_ps%d" % n) for n in range(NH // BANK)]
-        for n in range(NH // BANK):
-            nc.tensor.matmul(
-                h_ps[n][:], lhsT=ones[:], rhs=bias_rows[:, BANK * n : BANK * (n + 1)],
-                start=True, stop=False,
-            )
-        for block in range(LIN_BLOCKS):
-            b, j = divmod(block, PACK)
+            h_ps = [psum_h.tile([P, BANK], F32, name="h_ps%d" % n) for n in range(NH // BANK)]
             for n in range(NH // BANK):
                 nc.tensor.matmul(
-                    h_ps[n][:],
-                    lhsT=xT_sb[:, block, :],
-                    rhs=w_lin_sb[:, b, j, BANK * n : BANK * (n + 1)],
-                    start=False,
-                    stop=(block == LIN_BLOCKS - 1),
+                    h_ps[n][:], lhsT=ones[:], rhs=bias_rows[:, BANK * n : BANK * (n + 1)],
+                    start=True, stop=False,
                 )
-        h_sb = keep.tile([P, NH], BF16)
-        nc.scalar.activation(
-            out=h_sb[:, 0:BANK], in_=h_ps[0][:], func=mybir.ActivationFunctionType.Relu
-        )
-        nc.vector.tensor_scalar_max(out=h_sb[:, BANK:NH], in0=h_ps[1][:], scalar1=0.0)
+            for block in range(LIN_BLOCKS):
+                b, j = divmod(block, PACK)
+                for n in range(NH // BANK):
+                    nc.tensor.matmul(
+                        h_ps[n][:],
+                        lhsT=xT_sb[:, block, :],
+                        rhs=w_lin_sb[:, b, j, BANK * n : BANK * (n + 1)],
+                        start=False,
+                        stop=(block == LIN_BLOCKS - 1),
+                    )
+            h_sb = keep.tile([P, NH], BF16)
+            nc.scalar.activation(
+                out=h_sb[:, 0:BANK], in_=h_ps[0][:], func=mybir.ActivationFunctionType.Relu
+            )
+            nc.vector.tensor_scalar_max(out=h_sb[:, BANK:NH], in0=h_ps[1][:], scalar1=0.0)
 
-        h_cols = (
-            h_sb[:].rearrange("i (g p t) -> i g t p", p=P, t=PACK),
-            h_sb[:].rearrange("i (g t p) -> i g t p", p=P, t=PACK),
-        )
-        v_words = keep.tile([P, 2, CONTEXT, H_PASSES, SEQ], U32, align_bytes=64)
-        v_scales = keep.tile([P, 2, CONTEXT, H_PASSES, SEQ], U8, align_bytes=64)
-        for order in (BY_WORD, BY_TILE):
-            hT_ps = psum_flip.tile([P, H_PASSES, PACK, SEQ], BF16, tag="flip")
-            for g in range(H_PASSES):
-                for t in range(PACK):
-                    nc.tensor.transpose(hT_ps[:, g, t, :], h_cols[order][:, g, t, :], ident[:])
-            centre = v_grouped[:, order, 1]
-            if order == BY_WORD:
-                nc.vector.tensor_copy(out=centre, in_=hT_ps[:].rearrange("p g t i -> p g i t"))
-            else:
-                nc.scalar.copy(out=centre, in_=hT_ps[:].rearrange("p g t i -> p g i t"))
-            nc.vector.tensor_copy(
-                out=v_grouped[:, order, 0, :, 1:SEQ, :], in_=centre[:, :, 0 : SEQ - 1, :]
+            h_cols = (
+                h_sb[:].rearrange("i (g p t) -> i g t p", p=P, t=PACK),
+                h_sb[:].rearrange("i (g t p) -> i g t p", p=P, t=PACK),
             )
-            nc.vector.tensor_copy(
-                out=v_grouped[:, order, 2, :, 0 : SEQ - 1, :], in_=centre[:, :, 1:SEQ, :]
-            )
-            for c in range(CONTEXT):
-                nc.vector.quantize_mx(
-                    out=v_words[:, order, c].rearrange("p g i -> p (g i)").bitcast(FP8X4),
-                    scales=v_scales[:, order, c].rearrange("p g i -> p (g i)"),
-                    in_=v_grouped[:, order, c].rearrange("p g i t -> p (g i t)"),
+            v_words = keep.tile([P, 2, CONTEXT, H_PASSES, SEQ], U32, align_bytes=64)
+            v_scales = keep.tile([P, 2, CONTEXT, H_PASSES, SEQ], U8, align_bytes=64)
+            for order in (BY_WORD, BY_TILE):
+                hT_ps = psum_flip.tile([P, H_PASSES, PACK, SEQ], BF16, tag="flip")
+                for g in range(H_PASSES):
+                    for t in range(PACK):
+                        nc.tensor.transpose(hT_ps[:, g, t, :], h_cols[order][:, g, t, :], ident[:])
+                centre = v_grouped[:, order, 1]
+                if order == BY_WORD:
+                    nc.vector.tensor_copy(out=centre, in_=hT_ps[:].rearrange("p g t i -> p g i t"))
+                else:
+                    nc.scalar.copy(out=centre, in_=hT_ps[:].rearrange("p g t i -> p g i t"))
+                nc.vector.tensor_copy(
+                    out=v_grouped[:, order, 0, :, 1:SEQ, :], in_=centre[:, :, 0 : SEQ - 1, :]
                 )
+                nc.vector.tensor_copy(
+                    out=v_grouped[:, order, 2, :, 0 : SEQ - 1, :], in_=centre[:, :, 1:SEQ, :]
+                )
+                for c in range(CONTEXT):
+                    nc.vector.quantize_mx(
+                        out=v_words[:, order, c].rearrange("p g i -> p (g i)").bitcast(FP8X4),
+                        scales=v_scales[:, order, c].rearrange("p g i -> p (g i)"),
+                        in_=v_grouped[:, order, c].rearrange("p g i t -> p (g i t)"),
+                    )
 
+        psum_t = ctx.enter_context(tc.psum_pool(name="psum_t", bufs=UNITS))
+        psum_out = ctx.enter_context(tc.psum_pool(name="psum_out", bufs=1))
         out_ps = psum_out.tile([P, NO, SEQ], F32)
 
-        def first_product(o, unit):
-            w_sb, first = w_of_unit[(o, unit)]
-            tT_ps = psum_t.tile([P, PACK, SEQ], F32)
+        def first_product(o, kp, unit, tT_ps):
+            c, g = divmod(kp, H_PASSES)
+            group = V_PASSES * o + kp
+            a, q = divmod(group, PLANES_PER_TILE)
+            w_sb, first = w_of[(group, unit)]
             for m in range(PACK):
                 col = K_PASS * unit + P * m
                 byte = (col - K_PASS * first) * PACK
-                for kp in range(V_PASSES):
-                    c, g = divmod(kp, H_PASSES)
-                    a, q = divmod(V_PASSES * o + kp, PLANES_PER_TILE)
-                    nc.tensor.matmul_mx(
-                        out=tT_ps[:, m, :],
-                        lhsT=w_sb[:, kp, byte : byte + P * PACK].bitcast(FP8X4),
-                        lhsT_scale=planes[4 * q : P, a, col : col + P],
-                        rhs=v_words[:, BY_WORD, c, g, :].bitcast(FP8X4),
-                        rhs_scale=v_scales[:, BY_WORD, c, g, :],
-                        start=(kp == 0),
-                        stop=(kp == V_PASSES - 1),
-                    )
-            return tT_ps
+                nc.tensor.matmul_mx(
+                    out=tT_ps[:, m, :],
+                    lhsT=w_sb[:, byte : byte + P * PACK].bitcast(FP8X4),
+                    lhsT_scale=planes[4 * q : P, a, col : col + P],
+                    rhs=v_words[:, BY_WORD, c, g, :].bitcast(FP8X4),
+                    rhs_scale=v_scales[:, BY_WORD, c, g, :],
+                    start=(kp == 0 and m == 0),
+                    stop=(kp == V_PASSES - 1 and m == PACK - 1),
+                )
 
-        def quantise_t(tT_ps):
+        def quantise_t(unit, tT_ps):
             t_grouped = stage.tile([P, SEQ, PACK], BF16, align_bytes=64)
-            nc.scalar.copy(out=t_grouped[:], in_=tT_ps[:].rearrange("p m i -> p i m"))
+            if unit % 2 == 0:
+                nc.scalar.copy(out=t_grouped[:], in_=tT_ps[:].rearrange("p m i -> p i m"))
+            else:
+                nc.vector.tensor_copy(out=t_grouped[:], in_=tT_ps[:].rearrange("p m i -> p i m"))
             t_words = stage.tile([P, SEQ], U32, align_bytes=64)
             t_scales = stage.tile([P, SEQ], U8, align_bytes=64)
             nc.vector.quantize_mx(
@@ -221,15 +210,19 @@ def tile_bilinearpairedlayer_w_e_kernel(
                 stop=(unit == UNITS - 1),
             )
 
-        waiting = None
         for o in range(NO):
+            banks = [psum_t.tile([P, PACK, SEQ], F32, name="tT_ps", tag="tT") for unit in range(UNITS)]
+            for kp in range(V_PASSES - 1):
+                for unit in range(UNITS):
+                    first_product(o, kp, unit, banks[unit])
+            waiting = None
             for unit in range(UNITS):
-                tT_ps = first_product(o, unit)
-                t_words, t_scales = quantise_t(tT_ps)
+                first_product(o, V_PASSES - 1, unit, banks[unit])
+                t_words, t_scales = quantise_t(unit, banks[unit])
                 if waiting is not None:
                     second_product(*waiting)
                 waiting = (o, unit, t_words, t_scales)
-        second_product(*waiting)
+            second_product(*waiting)
 
         result = keep.tile([P, SEQ, NO], F32)
         nc.vector.tensor_tensor(

@@ -55,7 +55,7 @@ def tile_bilinearpairedlayer_w_e_kernel(
         nc.vector.memset(v_grouped[:, :, 2, :, SEQ - 1, :], 0.0)
 
         x_sb = keep.tile([P, NI], BF16)
-        nc.sync.dma_start(out=x_sb[:], in_=x[0])
+        nc.scalar.dma_start(out=x_sb[:], in_=x[0])
         nc.scalar.dma_start(out=bias_rows[0:1, :], in_=b_lin.unsqueeze(0))
         b_bil_bf = keep.tile([P, NO], BF16)
         nc.scalar.dma_start(out=b_bil_bf[:], in_=b_bil.partition_broadcast(P))
@@ -64,19 +64,18 @@ def tile_bilinearpairedlayer_w_e_kernel(
 
         w_lin_sb = keep.tile([P, NI // K_PASS, PACK, NH], BF16)
         for b in range(NI // K_PASS):
-            nc.sync.dma_start(
+            nc.scalar.dma_start(
                 out=w_lin_sb[:, b].rearrange("p j k -> p (j k)"),
                 in_=W_lin[K_PASS * b : K_PASS * (b + 1), :].rearrange("(p j) k -> p (j k)", j=PACK),
             )
-
-        for a in range(NO * V_PASSES // PLANES_PER_TILE):
-            for quad in range(4):
-                nc.sync.dma_start(
-                    out=planes[32 * quad : 32 * quad + 16, a, :].bitcast(I32),
-                    in_=W_bil_scales[
-                        PLANES_PER_TILE * a : PLANES_PER_TILE * (a + 1), 4 * quad : 4 * quad + 4, :
-                    ].bitcast(I32),
-                )
+            if b < NO * V_PASSES // PLANES_PER_TILE:
+                for quad in range(4):
+                    nc.sync.dma_start(
+                        out=planes[32 * quad : 32 * quad + 16, b, :].bitcast(I32),
+                        in_=W_bil_scales[
+                            PLANES_PER_TILE * b : PLANES_PER_TILE * (b + 1), 4 * quad : 4 * quad + 4, :
+                        ].bitcast(I32),
+                    )
 
         w_of = {}
         for group in range(NO * V_PASSES):

@@ -23,9 +23,12 @@ H = NH * CONTEXT
 
 H_PASSES = NH // K_PASS
 V_PASSES = H // K_PASS
+GROUPS = NO * V_PASSES
 UNITS = H // K_PASS
 LIN_BLOCKS = NI // P
 BANK = 512
+FLIPS_PER_BANK = 2 * BANK // SEQ
+QUADRANT = 32
 PLANES_PER_TILE = 4
 
 BY_WORD = 0
@@ -42,7 +45,7 @@ def tile_bilinearpairedlayer_w_e_kernel(
         keep = ctx.enter_context(tc.tile_pool(name="keep", bufs=1))
         stage = ctx.enter_context(tc.tile_pool(name="stage", bufs=3))
 
-        planes = keep.tile([P, NO * V_PASSES // PLANES_PER_TILE, H], U8, align_bytes=64)
+        planes = keep.tile([P, GROUPS // PLANES_PER_TILE, H], U8, align_bytes=64)
         nc.vector.memset(planes[:].rearrange("p a n -> p (a n)").bitcast(I32), 0)
         ident = keep.tile([P, P], BF16)
         make_identity(nc, ident[:])
@@ -55,7 +58,7 @@ def tile_bilinearpairedlayer_w_e_kernel(
         nc.vector.memset(v_grouped[:, :, 2, :, SEQ - 1, :], 0.0)
 
         x_sb = keep.tile([P, NI], BF16)
-        nc.scalar.dma_start(out=x_sb[:], in_=x[0])
+        nc.sync.dma_start(out=x_sb[:], in_=x[0])
         nc.scalar.dma_start(out=bias_rows[0:1, :], in_=b_lin.unsqueeze(0))
         b_bil_bf = keep.tile([P, NO], BF16)
         nc.scalar.dma_start(out=b_bil_bf[:], in_=b_bil.partition_broadcast(P))
@@ -64,22 +67,25 @@ def tile_bilinearpairedlayer_w_e_kernel(
 
         w_lin_sb = keep.tile([P, NI // K_PASS, PACK, NH], BF16)
         for b in range(NI // K_PASS):
-            nc.scalar.dma_start(
+            nc.sync.dma_start(
                 out=w_lin_sb[:, b].rearrange("p j k -> p (j k)"),
                 in_=W_lin[K_PASS * b : K_PASS * (b + 1), :].rearrange("(p j) k -> p (j k)", j=PACK),
             )
-            if b < NO * V_PASSES // PLANES_PER_TILE:
-                for quad in range(4):
-                    nc.sync.dma_start(
-                        out=planes[32 * quad : 32 * quad + 16, b, :].bitcast(I32),
-                        in_=W_bil_scales[
-                            PLANES_PER_TILE * b : PLANES_PER_TILE * (b + 1), 4 * quad : 4 * quad + 4, :
-                        ].bitcast(I32),
-                    )
+
+        for a in range(GROUPS // PLANES_PER_TILE):
+            for quad in (0, 2, 1, 3):
+                nc.sync.dma_start(
+                    out=planes[
+                        QUADRANT * quad : QUADRANT * quad + 4 * PLANES_PER_TILE, a, :
+                    ].bitcast(I32),
+                    in_=W_bil_scales[
+                        PLANES_PER_TILE * a : PLANES_PER_TILE * (a + 1), 4 * quad : 4 * quad + 4, :
+                    ].bitcast(I32),
+                )
 
         w_of = {}
-        for group in range(NO * V_PASSES):
-            units = 1 if group == NO * V_PASSES - 1 else UNITS
+        for group in range(GROUPS):
+            units = 1 if group == GROUPS - 1 else UNITS
             for first in range(0, UNITS, units):
                 w_sb = keep.tile(
                     [P, units * K_PASS * PACK], U8, name="w_%d_%d" % (group, first), align_bytes=64
@@ -98,16 +104,16 @@ def tile_bilinearpairedlayer_w_e_kernel(
         ) as psum_h:
             x_cols = x_sb[:].rearrange("i (b p j) -> i b j p", p=P, j=PACK)
             xT_sb = keep.tile([P, LIN_BLOCKS, SEQ], BF16)
-            per_bank = LIN_BLOCKS // 2
-            for half in range(2):
-                xT_ps = psum_flip.tile([P, per_bank, SEQ], BF16, tag="flip")
-                for s in range(per_bank):
-                    b, j = divmod(per_bank * half + s, PACK)
-                    nc.tensor.transpose(xT_ps[:, s, :], x_cols[:, b, j, :], ident[:])
-                if half == 0:
-                    nc.vector.tensor_copy(out=xT_sb[:, 0:per_bank, :], in_=xT_ps[:])
+            for bank in range(LIN_BLOCKS // FLIPS_PER_BANK):
+                xT_ps = psum_flip.tile([P, FLIPS_PER_BANK, SEQ], BF16, tag="flip")
+                for flip in range(FLIPS_PER_BANK):
+                    b, j = divmod(FLIPS_PER_BANK * bank + flip, PACK)
+                    nc.tensor.transpose(xT_ps[:, flip, :], x_cols[:, b, j, :], ident[:])
+                blocks = xT_sb[:, FLIPS_PER_BANK * bank : FLIPS_PER_BANK * (bank + 1), :]
+                if bank == 0:
+                    nc.vector.tensor_copy(out=blocks, in_=xT_ps[:])
                 else:
-                    nc.scalar.copy(out=xT_sb[:, per_bank:LIN_BLOCKS, :], in_=xT_ps[:])
+                    nc.scalar.copy(out=blocks, in_=xT_ps[:])
 
             h_ps = [psum_h.tile([P, BANK], F32, name="h_ps%d" % n) for n in range(NH // BANK)]
             for n in range(NH // BANK):
@@ -132,21 +138,21 @@ def tile_bilinearpairedlayer_w_e_kernel(
             nc.vector.tensor_scalar_max(out=h_sb[:, BANK:NH], in0=h_ps[1][:], scalar1=0.0)
 
             h_cols = (
-                h_sb[:].rearrange("i (g p t) -> i g t p", p=P, t=PACK),
-                h_sb[:].rearrange("i (g t p) -> i g t p", p=P, t=PACK),
+                h_sb[:].rearrange("i (f p s) -> i f s p", p=P, s=PACK),
+                h_sb[:].rearrange("i (f s p) -> i f s p", p=P, s=PACK),
             )
             v_words = keep.tile([P, 2, CONTEXT, H_PASSES, SEQ], U32, align_bytes=64)
             v_scales = keep.tile([P, 2, CONTEXT, H_PASSES, SEQ], U8, align_bytes=64)
             for order in (BY_WORD, BY_TILE):
                 hT_ps = psum_flip.tile([P, H_PASSES, PACK, SEQ], BF16, tag="flip")
-                for g in range(H_PASSES):
-                    for t in range(PACK):
-                        nc.tensor.transpose(hT_ps[:, g, t, :], h_cols[order][:, g, t, :], ident[:])
+                for f in range(H_PASSES):
+                    for s in range(PACK):
+                        nc.tensor.transpose(hT_ps[:, f, s, :], h_cols[order][:, f, s, :], ident[:])
                 centre = v_grouped[:, order, 1]
                 if order == BY_WORD:
-                    nc.vector.tensor_copy(out=centre, in_=hT_ps[:].rearrange("p g t i -> p g i t"))
+                    nc.vector.tensor_copy(out=centre, in_=hT_ps[:].rearrange("p f s i -> p f i s"))
                 else:
-                    nc.scalar.copy(out=centre, in_=hT_ps[:].rearrange("p g t i -> p g i t"))
+                    nc.scalar.copy(out=centre, in_=hT_ps[:].rearrange("p f s i -> p f i s"))
                 nc.vector.tensor_copy(
                     out=v_grouped[:, order, 0, :, 1:SEQ, :], in_=centre[:, :, 0 : SEQ - 1, :]
                 )
@@ -155,19 +161,19 @@ def tile_bilinearpairedlayer_w_e_kernel(
                 )
                 for c in range(CONTEXT):
                     nc.vector.quantize_mx(
-                        out=v_words[:, order, c].rearrange("p g i -> p (g i)").bitcast(FP8X4),
-                        scales=v_scales[:, order, c].rearrange("p g i -> p (g i)"),
-                        in_=v_grouped[:, order, c].rearrange("p g i t -> p (g i t)"),
+                        out=v_words[:, order, c].rearrange("p f i -> p (f i)").bitcast(FP8X4),
+                        scales=v_scales[:, order, c].rearrange("p f i -> p (f i)"),
+                        in_=v_grouped[:, order, c].rearrange("p f i s -> p (f i s)"),
                     )
 
         psum_t = ctx.enter_context(tc.psum_pool(name="psum_t", bufs=UNITS))
         psum_out = ctx.enter_context(tc.psum_pool(name="psum_out", bufs=1))
         out_ps = psum_out.tile([P, NO, SEQ], F32)
 
-        def first_product(o, kp, unit, tT_ps):
-            c, g = divmod(kp, H_PASSES)
-            group = V_PASSES * o + kp
-            a, q = divmod(group, PLANES_PER_TILE)
+        def first_product(o, v_pass, unit, tT_ps):
+            c, f = divmod(v_pass, H_PASSES)
+            group = V_PASSES * o + v_pass
+            a, slot = divmod(group, PLANES_PER_TILE)
             w_sb, first = w_of[(group, unit)]
             for m in range(PACK):
                 col = K_PASS * unit + P * m
@@ -175,16 +181,16 @@ def tile_bilinearpairedlayer_w_e_kernel(
                 nc.tensor.matmul_mx(
                     out=tT_ps[:, m, :],
                     lhsT=w_sb[:, byte : byte + P * PACK].bitcast(FP8X4),
-                    lhsT_scale=planes[4 * q : P, a, col : col + P],
-                    rhs=v_words[:, BY_WORD, c, g, :].bitcast(FP8X4),
-                    rhs_scale=v_scales[:, BY_WORD, c, g, :],
-                    start=(kp == 0 and m == 0),
-                    stop=(kp == V_PASSES - 1 and m == PACK - 1),
+                    lhsT_scale=planes[4 * slot : P, a, col : col + P],
+                    rhs=v_words[:, BY_WORD, c, f, :].bitcast(FP8X4),
+                    rhs_scale=v_scales[:, BY_WORD, c, f, :],
+                    start=(v_pass == 0 and m == 0),
+                    stop=(v_pass == V_PASSES - 1 and m == PACK - 1),
                 )
 
         def quantise_t(unit, tT_ps):
             t_grouped = stage.tile([P, SEQ, PACK], BF16, align_bytes=64)
-            if unit % 2 == 0:
+            if unit % 2 == 1:
                 nc.scalar.copy(out=t_grouped[:], in_=tT_ps[:].rearrange("p m i -> p i m"))
             else:
                 nc.vector.tensor_copy(out=t_grouped[:], in_=tT_ps[:].rearrange("p m i -> p i m"))
@@ -198,22 +204,22 @@ def tile_bilinearpairedlayer_w_e_kernel(
             return t_words, t_scales
 
         def second_product(o, unit, t_words, t_scales):
-            c, g = divmod(unit, H_PASSES)
+            c, f = divmod(unit, H_PASSES)
             nc.tensor.matmul_mx(
                 out=out_ps[:, o, :],
                 lhsT=t_words[:].bitcast(FP8X4),
                 lhsT_scale=t_scales[:],
-                rhs=v_words[:, BY_TILE, c, g, :].bitcast(FP8X4),
-                rhs_scale=v_scales[:, BY_TILE, c, g, :],
+                rhs=v_words[:, BY_TILE, c, f, :].bitcast(FP8X4),
+                rhs_scale=v_scales[:, BY_TILE, c, f, :],
                 start=(unit == 0),
                 stop=(unit == UNITS - 1),
             )
 
         for o in range(NO):
             banks = [psum_t.tile([P, PACK, SEQ], F32, name="tT_ps", tag="tT") for unit in range(UNITS)]
-            for kp in range(V_PASSES - 1):
+            for v_pass in range(V_PASSES - 1):
                 for unit in range(UNITS):
-                    first_product(o, kp, unit, banks[unit])
+                    first_product(o, v_pass, unit, banks[unit])
             waiting = None
             for unit in range(UNITS):
                 first_product(o, V_PASSES - 1, unit, banks[unit])

@@ -49,7 +49,7 @@ def tile_bilinearpairedlayer_w_e_kernel(
         nc.vector.memset(planes[:].rearrange("p a n -> p (a n)").bitcast(I32), 0)
         ident = keep.tile([P, P], BF16)
         make_identity(nc, ident[:])
-        bias_rows = keep.tile([P, NH], BF16)
+        bias_rows = keep.tile([P, NH + QUADRANT], BF16)
         nc.gpsimd.memset(bias_rows[:], 0.0)
         ones = keep.tile([P, P], BF16)
         nc.gpsimd.memset(ones[:], 1.0)
@@ -59,11 +59,8 @@ def tile_bilinearpairedlayer_w_e_kernel(
 
         x_sb = keep.tile([P, NI], BF16)
         nc.sync.dma_start(out=x_sb[:], in_=x[0])
-        nc.scalar.dma_start(out=bias_rows[0:1, :], in_=b_lin.unsqueeze(0))
-        b_bil_bf = keep.tile([P, NO], BF16)
-        nc.scalar.dma_start(out=b_bil_bf[:], in_=b_bil.partition_broadcast(P))
-        b_bil_f32 = keep.tile([P, NO], F32)
-        nc.vector.tensor_copy(out=b_bil_f32[:], in_=b_bil_bf[:])
+        nc.scalar.dma_start(out=bias_rows[0:1, 0:NH], in_=b_lin.unsqueeze(0))
+        nc.scalar.dma_start(out=bias_rows[0:1, NH : NH + NO], in_=b_bil.unsqueeze(0))
 
         w_lin_sb = keep.tile([P, NI // K_PASS, PACK, NH], BF16)
         for b in range(NI // K_PASS):
@@ -116,11 +113,6 @@ def tile_bilinearpairedlayer_w_e_kernel(
                     nc.scalar.copy(out=blocks, in_=xT_ps[:])
 
             h_ps = [psum_h.tile([P, BANK], F32, name="h_ps%d" % n) for n in range(NH // BANK)]
-            for n in range(NH // BANK):
-                nc.tensor.matmul(
-                    h_ps[n][:], lhsT=ones[:], rhs=bias_rows[:, BANK * n : BANK * (n + 1)],
-                    start=True, stop=False,
-                )
             for block in range(LIN_BLOCKS):
                 b, j = divmod(block, PACK)
                 for n in range(NH // BANK):
@@ -128,9 +120,20 @@ def tile_bilinearpairedlayer_w_e_kernel(
                         h_ps[n][:],
                         lhsT=xT_sb[:, block, :],
                         rhs=w_lin_sb[:, b, j, BANK * n : BANK * (n + 1)],
-                        start=False,
-                        stop=(block == LIN_BLOCKS - 1),
+                        start=(block == 0),
+                        stop=False,
                     )
+            for n in range(NH // BANK):
+                nc.tensor.matmul(
+                    h_ps[n][:], lhsT=ones[:], rhs=bias_rows[:, BANK * n : BANK * (n + 1)],
+                    start=False, stop=True,
+                )
+            b_bil_ps = psum_h.tile([P, NO], F32)
+            nc.tensor.matmul(
+                b_bil_ps[:], lhsT=ones[:], rhs=bias_rows[:, NH : NH + NO], start=True, stop=True
+            )
+            b_bil_f32 = keep.tile([P, NO], F32)
+            nc.vector.tensor_copy(out=b_bil_f32[:], in_=b_bil_ps[:])
             h_sb = keep.tile([P, NH], BF16)
             nc.scalar.activation(
                 out=h_sb[:, 0:BANK], in_=h_ps[0][:], func=mybir.ActivationFunctionType.Relu

@@ -171,6 +171,7 @@ def tile_bilinearpairedlayer_w_e_kernel(
 
         psum_t = ctx.enter_context(tc.psum_pool(name="psum_t", bufs=UNITS))
         psum_out = ctx.enter_context(tc.psum_pool(name="psum_out", bufs=1))
+        psum_turn = ctx.enter_context(tc.psum_pool(name="psum_turn", bufs=1))
         out_ps = psum_out.tile([P, NO, SEQ], F32)
 
         def first_product(o, v_pass, unit, tT_ps):
@@ -190,6 +191,36 @@ def tile_bilinearpairedlayer_w_e_kernel(
                     start=(v_pass == 0 and m == 0),
                     stop=(v_pass == V_PASSES - 1 and m == PACK - 1),
                 )
+
+        def first_product_rows(v_pass, unit, t_ps):
+            c, f = divmod(v_pass, H_PASSES)
+            a, slot = divmod(v_pass, PLANES_PER_TILE)
+            w_sb, first = w_of[(v_pass, unit)]
+            byte = K_PASS * (unit - first) * PACK
+            nc.tensor.matmul_mx(
+                out=t_ps[:].rearrange("p m i -> p (m i)"),
+                lhsT=v_words[:, BY_WORD, c, f, :].bitcast(FP8X4),
+                lhsT_scale=v_scales[:, BY_WORD, c, f, :],
+                rhs=w_sb[:, byte : byte + K_PASS * PACK].bitcast(FP8X4),
+                rhs_scale=planes[4 * slot : P, a, K_PASS * unit : K_PASS * (unit + 1)],
+                start=(v_pass == 0),
+                stop=(v_pass == V_PASSES - 1),
+            )
+
+        def round_rows(unit, t_ps):
+            t_rows = stage.tile([P, K_PASS], BF16)
+            rows = t_ps[:].rearrange("p m i -> p (m i)")
+            if unit % 2 == 1:
+                nc.scalar.copy(out=t_rows[:], in_=rows)
+            else:
+                nc.vector.tensor_copy(out=t_rows[:], in_=rows)
+            return t_rows
+
+        def turn_and_quantise(unit, t_rows):
+            turn_ps = psum_turn.tile([P, PACK, SEQ], BF16)
+            for m in range(PACK):
+                nc.tensor.transpose(turn_ps[:, m, :], t_rows[:, P * m : P * (m + 1)], ident[:])
+            return quantise_t(unit + 1, turn_ps)
 
         def quantise_t(unit, tT_ps):
             t_grouped = stage.tile([P, SEQ, PACK], BF16, align_bytes=64)
@@ -218,7 +249,21 @@ def tile_bilinearpairedlayer_w_e_kernel(
                 stop=(unit == UNITS - 1),
             )
 
-        for o in range(NO):
+        banks = [psum_t.tile([P, PACK, SEQ], F32, name="tT_ps", tag="tT") for unit in range(UNITS)]
+        for v_pass in range(V_PASSES - 1):
+            for unit in range(UNITS):
+                first_product_rows(v_pass, unit, banks[unit])
+        rows, turned = {}, {}
+        for step in range(UNITS + 2):
+            if step < UNITS:
+                first_product_rows(V_PASSES - 1, step, banks[step])
+                rows[step] = round_rows(step, banks[step])
+            if 0 <= step - 1 < UNITS:
+                turned[step - 1] = turn_and_quantise(step - 1, rows[step - 1])
+            if 0 <= step - 2 < UNITS:
+                second_product(0, step - 2, *turned[step - 2])
+
+        for o in range(1, NO):
             banks = [psum_t.tile([P, PACK, SEQ], F32, name="tT_ps", tag="tT") for unit in range(UNITS)]
             for v_pass in range(V_PASSES - 1):
                 for unit in range(UNITS):

@@ -69,8 +69,8 @@ def tile_bilinearpairedlayer_w_e_kernel(
                 in_=W_lin[K_PASS * b : K_PASS * (b + 1), :].rearrange("(p j) k -> p (j k)", j=PACK),
             )
 
-        for a in range(GROUPS // PLANES_PER_TILE):
-            for quad in (0, 2, 1, 3):
+        for quad in (2, 3, 0, 1):
+            for a in range(GROUPS // PLANES_PER_TILE):
                 nc.sync.dma_start(
                     out=planes[
                         QUADRANT * quad : QUADRANT * quad + 4 * PLANES_PER_TILE, a, :

from contextlib import ExitStack

import concourse.mybir as mybir
from concourse.masks import make_identity

BF16 = mybir.dt.bfloat16
F32 = mybir.dt.float32
I32 = mybir.dt.int32
U32 = mybir.dt.uint32
U8 = mybir.dt.uint8
FP8X4 = mybir.dt.float8_e4m3fn_x4

P = 128
PACK = 4
K_PASS = P * PACK

SEQ = 128
NI = 2048
NH = 1024
NO = 2
CONTEXT = 3
H = NH * CONTEXT

H_PASSES = NH // K_PASS
V_PASSES = H // K_PASS
GROUPS = NO * V_PASSES
UNITS = H // K_PASS
LIN_BLOCKS = NI // P
BANK = 512
FLIPS_PER_BANK = 2 * BANK // SEQ
QUADRANT = 32
PLANES_PER_TILE = 4

BY_WORD = 0
BY_TILE = 1

FLOPS = 2 * SEQ * NI * NH + 2 * SEQ * H * H * NO + 2 * SEQ * SEQ * H * NO


def tile_bilinearpairedlayer_w_e_kernel(
    tc, x, W_lin, b_lin, W_bil_words, W_bil_scales, b_bil, out
):
    nc = tc.nc
    with ExitStack() as ctx:
        keep = ctx.enter_context(tc.tile_pool(name="keep", bufs=1))
        stage = ctx.enter_context(tc.tile_pool(name="stage", bufs=3))

        planes = keep.tile([P, GROUPS // PLANES_PER_TILE, H], U8, align_bytes=64)
        nc.vector.memset(planes[:].rearrange("p a n -> p (a n)").bitcast(I32), 0)
        ident = keep.tile([P, P], BF16)
        make_identity(nc, ident[:])
        bias_rows = keep.tile([P, NH + QUADRANT], BF16)
        nc.gpsimd.memset(bias_rows[:], 0.0)
        ones = keep.tile([P, P], BF16)
        nc.gpsimd.memset(ones[:], 1.0)
        v_grouped = keep.tile([P, 2, CONTEXT, H_PASSES, SEQ, PACK], BF16, align_bytes=64)
        nc.vector.memset(v_grouped[:, :, 0, :, 0, :], 0.0)
        nc.vector.memset(v_grouped[:, :, 2, :, SEQ - 1, :], 0.0)

        x_sb = keep.tile([P, NI], BF16)
        nc.sync.dma_start(out=x_sb[:], in_=x[0])
        nc.scalar.dma_start(out=bias_rows[0:1, 0:NH], in_=b_lin.unsqueeze(0))
        nc.scalar.dma_start(out=bias_rows[0:1, NH : NH + NO], in_=b_bil.unsqueeze(0))

        w_lin_sb = keep.tile([P, NI // K_PASS, PACK, NH], BF16)
        for b in range(NI // K_PASS):
            nc.sync.dma_start(
                out=w_lin_sb[:, b].rearrange("p j k -> p (j k)"),
                in_=W_lin[K_PASS * b : K_PASS * (b + 1), :].rearrange("(p j) k -> p (j k)", j=PACK),
            )

        for quad in (2, 3, 0, 1):
            for a in range(GROUPS // PLANES_PER_TILE):
                nc.sync.dma_start(
                    out=planes[
                        QUADRANT * quad : QUADRANT * quad + 4 * PLANES_PER_TILE, a, :
                    ].bitcast(I32),
                    in_=W_bil_scales[
                        PLANES_PER_TILE * a : PLANES_PER_TILE * (a + 1), 4 * quad : 4 * quad + 4, :
                    ].bitcast(I32),
                )

        w_of = {}
        for group in range(GROUPS):
            units = 1 if group == GROUPS - 1 else UNITS
            for first in range(0, UNITS, units):
                w_sb = keep.tile(
                    [P, units * K_PASS * PACK], U8, name="w_%d_%d" % (group, first), align_bytes=64
                )
                nc.sync.dma_start(
                    out=w_sb[:].bitcast(I32),
                    in_=W_bil_words[group].rearrange("p n t -> p (n t)")[
                        :, first * K_PASS * PACK : (first + units) * K_PASS * PACK
                    ].bitcast(I32),
                )
                for unit in range(first, first + units):
                    w_of[(group, unit)] = (w_sb, first)

        with tc.psum_pool(name="psum_flip", bufs=2) as psum_flip, tc.psum_pool(
            name="psum_h", bufs=1
        ) as psum_h:
            x_cols = x_sb[:].rearrange("i (b p j) -> i b j p", p=P, j=PACK)
            xT_sb = keep.tile([P, LIN_BLOCKS, SEQ], BF16)
            for bank in range(LIN_BLOCKS // FLIPS_PER_BANK):
                xT_ps = psum_flip.tile([P, FLIPS_PER_BANK, SEQ], BF16, tag="flip")
                for flip in range(FLIPS_PER_BANK):
                    b, j = divmod(FLIPS_PER_BANK * bank + flip, PACK)
                    nc.tensor.transpose(xT_ps[:, flip, :], x_cols[:, b, j, :], ident[:])
                blocks = xT_sb[:, FLIPS_PER_BANK * bank : FLIPS_PER_BANK * (bank + 1), :]
                if bank == 0:
                    nc.vector.tensor_copy(out=blocks, in_=xT_ps[:])
                else:
                    nc.scalar.copy(out=blocks, in_=xT_ps[:])

            h_ps = [psum_h.tile([P, BANK], F32, name="h_ps%d" % n) for n in range(NH // BANK)]
            for block in range(LIN_BLOCKS):
                b, j = divmod(block, PACK)
                for n in range(NH // BANK):
                    nc.tensor.matmul(
                        h_ps[n][:],
                        lhsT=xT_sb[:, block, :],
                        rhs=w_lin_sb[:, b, j, BANK * n : BANK * (n + 1)],
                        start=(block == 0),
                        stop=False,
                    )
            for n in range(NH // BANK):
                nc.tensor.matmul(
                    h_ps[n][:], lhsT=ones[:], rhs=bias_rows[:, BANK * n : BANK * (n + 1)],
                    start=False, stop=True,
                )
            b_bil_ps = psum_h.tile([P, NO], F32)
            nc.tensor.matmul(
                b_bil_ps[:], lhsT=ones[:], rhs=bias_rows[:, NH : NH + NO], start=True, stop=True
            )
            b_bil_f32 = keep.tile([P, NO], F32)
            nc.vector.tensor_copy(out=b_bil_f32[:], in_=b_bil_ps[:])
            h_sb = keep.tile([P, NH], BF16)
            nc.scalar.activation(
                out=h_sb[:, 0:BANK], in_=h_ps[0][:], func=mybir.ActivationFunctionType.Relu
            )
            nc.vector.tensor_scalar_max(out=h_sb[:, BANK:NH], in0=h_ps[1][:], scalar1=0.0)

            h_cols = (
                h_sb[:].rearrange("i (f p s) -> i f s p", p=P, s=PACK),
                h_sb[:].rearrange("i (f s p) -> i f s p", p=P, s=PACK),
            )
            v_words = keep.tile([P, 2, CONTEXT, H_PASSES, SEQ], U32, align_bytes=64)
            v_scales = keep.tile([P, 2, CONTEXT, H_PASSES, SEQ], U8, align_bytes=64)
            for order in (BY_WORD, BY_TILE):
                hT_ps = psum_flip.tile([P, H_PASSES, PACK, SEQ], BF16, tag="flip")
                for f in range(H_PASSES):
                    for s in range(PACK):
                        nc.tensor.transpose(hT_ps[:, f, s, :], h_cols[order][:, f, s, :], ident[:])
                centre = v_grouped[:, order, 1]
                if order == BY_WORD:
                    nc.vector.tensor_copy(out=centre, in_=hT_ps[:].rearrange("p f s i -> p f i s"))
                else:
                    nc.scalar.copy(out=centre, in_=hT_ps[:].rearrange("p f s i -> p f i s"))
                nc.vector.tensor_copy(
                    out=v_grouped[:, order, 0, :, 1:SEQ, :], in_=centre[:, :, 0 : SEQ - 1, :]
                )
                nc.vector.tensor_copy(
                    out=v_grouped[:, order, 2, :, 0 : SEQ - 1, :], in_=centre[:, :, 1:SEQ, :]
                )
                for c in range(CONTEXT):
                    nc.vector.quantize_mx(
                        out=v_words[:, order, c].rearrange("p f i -> p (f i)").bitcast(FP8X4),
                        scales=v_scales[:, order, c].rearrange("p f i -> p (f i)"),
                        in_=v_grouped[:, order, c].rearrange("p f i s -> p (f i s)"),
                    )

        psum_t = ctx.enter_context(tc.psum_pool(name="psum_t", bufs=UNITS))
        psum_out = ctx.enter_context(tc.psum_pool(name="psum_out", bufs=1))
        psum_turn = ctx.enter_context(tc.psum_pool(name="psum_turn", bufs=1))
        out_ps = psum_out.tile([P, NO, SEQ], F32)

        def first_product(o, v_pass, unit, tT_ps):
            c, f = divmod(v_pass, H_PASSES)
            group = V_PASSES * o + v_pass
            a, slot = divmod(group, PLANES_PER_TILE)
            w_sb, first = w_of[(group, unit)]
            for m in range(PACK):
                col = K_PASS * unit + P * m
                byte = (col - K_PASS * first) * PACK
                nc.tensor.matmul_mx(
                    out=tT_ps[:, m, :],
                    lhsT=w_sb[:, byte : byte + P * PACK].bitcast(FP8X4),
                    lhsT_scale=planes[4 * slot : P, a, col : col + P],
                    rhs=v_words[:, BY_WORD, c, f, :].bitcast(FP8X4),
                    rhs_scale=v_scales[:, BY_WORD, c, f, :],
                    start=(v_pass == 0 and m == 0),
                    stop=(v_pass == V_PASSES - 1 and m == PACK - 1),
                )

        def first_product_rows(v_pass, unit, t_ps):
            c, f = divmod(v_pass, H_PASSES)
            a, slot = divmod(v_pass, PLANES_PER_TILE)
            w_sb, first = w_of[(v_pass, unit)]
            byte = K_PASS * (unit - first) * PACK
            nc.tensor.matmul_mx(
                out=t_ps[:].rearrange("p m i -> p (m i)"),
                lhsT=v_words[:, BY_WORD, c, f, :].bitcast(FP8X4),
                lhsT_scale=v_scales[:, BY_WORD, c, f, :],
                rhs=w_sb[:, byte : byte + K_PASS * PACK].bitcast(FP8X4),
                rhs_scale=planes[4 * slot : P, a, K_PASS * unit : K_PASS * (unit + 1)],
                start=(v_pass == 0),
                stop=(v_pass == V_PASSES - 1),
            )

        def round_rows(unit, t_ps):
            t_rows = stage.tile([P, K_PASS], BF16)
            rows = t_ps[:].rearrange("p m i -> p (m i)")
            if unit % 2 == 1:
                nc.scalar.copy(out=t_rows[:], in_=rows)
            else:
                nc.vector.tensor_copy(out=t_rows[:], in_=rows)
            return t_rows

        def turn_and_quantise(unit, t_rows):
            turn_ps = psum_turn.tile([P, PACK, SEQ], BF16)
            for m in range(PACK):
                nc.tensor.transpose(turn_ps[:, m, :], t_rows[:, P * m : P * (m + 1)], ident[:])
            return quantise_t(unit + 1, turn_ps)

        def quantise_t(unit, tT_ps):
            t_grouped = stage.tile([P, SEQ, PACK], BF16, align_bytes=64)
            if unit % 2 == 1:
                nc.scalar.copy(out=t_grouped[:], in_=tT_ps[:].rearrange("p m i -> p i m"))
            else:
                nc.vector.tensor_copy(out=t_grouped[:], in_=tT_ps[:].rearrange("p m i -> p i m"))
            t_words = stage.tile([P, SEQ], U32, align_bytes=64)
            t_scales = stage.tile([P, SEQ], U8, align_bytes=64)
            nc.vector.quantize_mx(
                out=t_words[:].bitcast(FP8X4),
                scales=t_scales[:],
                in_=t_grouped[:].rearrange("p i m -> p (i m)"),
            )
            return t_words, t_scales

        def second_product(o, unit, t_words, t_scales):
            c, f = divmod(unit, H_PASSES)
            nc.tensor.matmul_mx(
                out=out_ps[:, o, :],
                lhsT=t_words[:].bitcast(FP8X4),
                lhsT_scale=t_scales[:],
                rhs=v_words[:, BY_TILE, c, f, :].bitcast(FP8X4),
                rhs_scale=v_scales[:, BY_TILE, c, f, :],
                start=(unit == 0),
                stop=(unit == UNITS - 1),
            )

        banks = [psum_t.tile([P, PACK, SEQ], F32, name="tT_ps", tag="tT") for unit in range(UNITS)]
        for v_pass in range(V_PASSES - 1):
            for unit in range(UNITS):
                first_product_rows(v_pass, unit, banks[unit])
        rows, turned = {}, {}
        for step in range(UNITS + 2):
            if step < UNITS:
                first_product_rows(V_PASSES - 1, step, banks[step])
                rows[step] = round_rows(step, banks[step])
            if 0 <= step - 1 < UNITS:
                turned[step - 1] = turn_and_quantise(step - 1, rows[step - 1])
            if 0 <= step - 2 < UNITS:
                second_product(0, step - 2, *turned[step - 2])

        for o in range(1, NO):
            banks = [psum_t.tile([P, PACK, SEQ], F32, name="tT_ps", tag="tT") for unit in range(UNITS)]
            for v_pass in range(V_PASSES - 1):
                for unit in range(UNITS):
                    first_product(o, v_pass, unit, banks[unit])
            waiting = None
            for unit in range(UNITS):
                first_product(o, V_PASSES - 1, unit, banks[unit])
                t_words, t_scales = quantise_t(unit, banks[unit])
                if waiting is not None:
                    second_product(*waiting)
                waiting = (o, unit, t_words, t_scales)
            second_product(*waiting)

        result = keep.tile([P, SEQ, NO], F32)
        nc.vector.tensor_tensor(
            out=result[:],
            in0=out_ps[:].rearrange("i o j -> i j o"),
            in1=b_bil_f32[:].unsqueeze(1).to_broadcast([P, SEQ, NO]),
            op=mybir.AluOpType.add,
        )
        nc.sync.dma_start(
            out=out[0].rearrange("i j o -> i (j o)"), in_=result[:].rearrange("i j o -> i (j o)")
        )
